import numpy as np
import ml_dtypes


def mxq(x, axis, fmt="e4m3"):
    dtype, down = {"e4m3": (ml_dtypes.float8_e4m3fn, 7), "e5m2": (ml_dtypes.float8_e5m2, 14)}[fmt]
    v = np.moveaxis(np.asarray(x, np.float32).astype(ml_dtypes.bfloat16).astype(np.float64), axis, -1)
    blocks = v.reshape(v.shape[:-1] + (-1, 32))
    amax = np.abs(blocks).max(-1, keepdims=True)
    byte = np.maximum(np.where(amax > 0, np.frexp(amax)[1] - 1 + 127, 0) - down, 1)
    scale = np.exp2(byte - 127.0)
    codes = (blocks / scale).astype(np.float32).astype(dtype).astype(np.float64)
    return np.moveaxis((codes * scale).reshape(v.shape), -1, axis)


WIDE = False


def mx_kscale(k):
    if not WIDE:
        return np.ones(k)
    levels = np.array([10, -10, 5, -5, 0])
    if k % 512:
        return np.exp2(np.random.permutation(np.resize(levels, k // 32))).repeat(32)
    a = np.empty((k // 512, 16))
    for p in range(k // 512):
        a[p, :8] = np.random.permutation(np.resize(levels, 8))
        for g in range(8):
            far = levels[np.abs(levels - a[p, g]) >= 10]
            a[p, g + 8] = far[np.random.randint(len(far))]
    return np.exp2(a.ravel()).repeat(32)


BF16 = ml_dtypes.bfloat16


def bf(x):
    return np.asarray(x, np.float32).astype(BF16)


def f64(x):
    return np.asarray(x).astype(np.float64)


N, DIN, H1, H2, C, NC, G = 1024, 512, 512, 256, 128, 512, 8


def draw0():
    s, t = mx_kscale(N), mx_kscale(DIN)
    return {"F_": bf(np.random.uniform(size=(N, N)) * 2.0 / np.sqrt(N) * s),
            "X": bf(np.random.standard_normal((N, DIN)) / s[:, None] * t),
            "W1": bf(np.random.standard_normal((DIN, H1)) * 0.8 / np.sqrt(DIN) / t[:, None]),
            "b1": bf(np.random.standard_normal(H1) * 0.3)}


def core(F_, X, W1, b1):
    agg = mxq(f64(F_), 1, "e4m3") @ mxq(f64(X), 0, "e4m3")
    return np.tanh((mxq(agg, 1, "e4m3") @ mxq(f64(W1), 0, "e4m3")) + f64(b1))


def e4m3fn_bytes(y):
    return np.clip(np.asarray(y, np.float64), -448.0, 448.0).astype(np.float32).astype(ml_dtypes.float8_e4m3fn).view(np.uint8)


def e4m3fn_values(b):
    return np.asarray(b, np.uint8).view(ml_dtypes.float8_e4m3fn).astype(np.float64)


def setup_inputs():
    d = draw0()
    x0 = np.asarray(d['F_']).astype(np.float64)
    s = (np.max(np.abs(x0), axis=(0,), keepdims=True) / 448.0).astype(np.float32)
    out = {}
    for k, v in d.items():
        if k == 'F_':
            out['F__bytes'] = e4m3fn_bytes(x0 / s.astype(np.float64))
            out['F__scale'] = s
        else:
            out[k] = v
    return out


def reference(F__bytes, F__scale, X, W1, b1):
    return core(e4m3fn_values(F__bytes) * F__scale.astype(np.float64), X, W1, b1)

@@ -1,0 +1,283 @@
+from contextlib import ExitStack
+
+import concourse.mybir as mybir
+from concourse.masks import make_identity
+
+NODES, FEATS, HID = 1024, 512, 512
+FLOPS = 2 * NODES * NODES * FEATS + 2 * NODES * FEATS * HID
+
+F32 = mybir.dt.float32
+BF16 = mybir.dt.bfloat16
+U32 = mybir.dt.uint32
+U8 = mybir.dt.uint8
+FP8 = mybir.dt.float8_e4m3fn
+FP8X4 = mybir.dt.float8_e4m3fn_x4
+ACT = mybir.ActivationFunctionType
+ALU = mybir.AluOpType
+
+P = 128
+NB = 8
+NG = 2
+VIA_GPSIMD = (5,)
+
+
+def tile_controencodnet_pa_kernel(tc, f_bytes, f_scale, x, w1, b1, out):
+    nc = tc.nc
+    f_view = f_bytes.rearrange("(p b) k -> p b k", b=NB)
+    o_view = out.rearrange("(p b) h -> p b h", b=NB)
+
+    with ExitStack() as ctx:
+        keep = ctx.enter_context(tc.tile_pool(name="keep", bufs=1))
+        work = ctx.enter_context(tc.tile_pool(name="work", bufs=3))
+        pst = ctx.enter_context(tc.psum_pool(name="pst", bufs=2))
+        psa = ctx.enter_context(tc.psum_pool(name="psa", bufs=2))
+        pso = ctx.enter_context(tc.psum_pool(name="pso", bufs=4))
+        ctx.enter_context(tc.manual_schedule())
+
+        raw = [keep.tile([P, 1, NODES], U8, name="raw0"), keep.tile([P, 1, NODES], U8, name="raw1")]
+        raw += [keep.tile([P, 2, NODES], U8, name="raw%d" % i) for i in (2, 4, 6)]
+
+        def bytes_of(b):
+            if b < 2:
+                return raw[b][:, 0, :]
+            return raw[1 + b // 2][:, b % 2, :]
+
+        scale = keep.tile([P, NG, 2, 2], F32)
+        nc.scalar.dma_start(
+            out=scale[:].rearrange("p g u e -> p g (u e)"),
+            in_=f_scale.rearrange("o (g p t) -> p (o g) t", p=P, t=4),
+        )
+        dummy = keep.tile([P, 1], F32)
+        dummy2 = keep.tile([P, 1], F32)
+        nc.vector.memset(dummy[:], 0.0)
+        nc.scalar.activation(out=dummy2[:], in_=dummy[:], func=ACT.Tanh)
+
+        nc.sync.dma_start(out=raw[0][:], in_=f_view[:, 0:1, :])
+        nc.sync.dma_start(out=raw[1][:], in_=f_view[:, 1:2, :])
+        nc.sync.dma_start(out=raw[2][:], in_=f_view[:, 2:4, :])
+        x_raw = [keep.tile([P, 4, FEATS], BF16, name="x_raw%d" % g) for g in range(NG)]
+        x_view = x.rearrange("(g p j) n -> g p j n", p=P, j=4)
+        for g in range(NG):
+            nc.sync.dma_start(out=x_raw[g][:], in_=x_view[g])
+        nc.sync.dma_start(out=raw[3][:], in_=f_view[:, 4:6, :])
+        nc.sync.dma_start(out=raw[4][:], in_=f_view[:, 6:8, :])
+        w_raw = keep.tile([P, 4, HID], BF16)
+        nc.sync.dma_start(out=w_raw[:], in_=w1.rearrange("(p j) n -> p j n", j=4))
+        bias = keep.tile([P, HID], BF16)
+        nc.sync.dma_start(out=bias[:], in_=b1.partition_broadcast(P))
+
+        ident = keep.tile([P, P], F32)
+        make_identity(nc, ident[:])
+
+        x_codes = [keep.tile([P, FEATS], U32, name="x_codes%d" % g, align_bytes=64) for g in range(NG)]
+        x_scales = [keep.tile([P, FEATS], U8, name="x_scales%d" % g, align_bytes=64) for g in range(NG)]
+        x_grp = [keep.tile([P, 4, P, 4], BF16, name="x_grp%d" % g, align_bytes=64) for g in range(NG)]
+        w_codes = keep.tile([P, HID], U32, align_bytes=64)
+        w_scales = keep.tile([P, HID], U8, align_bytes=64)
+        w_grp = keep.tile([P, 4 * HID], BF16, align_bytes=64)
+
+        st = {}
+
+        def cast(b):
+            t = work.tile([P, NODES], BF16, name="f_bf", align_bytes=64, bufs=6)
+            if b < 2:
+                nc.vector.tensor_copy(out=t[:], in_=bytes_of(b).bitcast(FP8))
+            else:
+                nc.scalar.copy(out=t[:], in_=bytes_of(b).bitcast(FP8))
+            st["c", b] = t
+
+        def turn(b):
+            t = pst.tile([P, 2, NG, P], F32, name="f_t")
+            words = st["c", b][:].bitcast(F32)
+            for g in range(NG):
+                for u in range(2):
+                    nc.tensor.transpose(t[:, u, g, :], words[:, 256 * g + u : 256 * (g + 1) : 2], ident[:])
+            st["t", b] = t
+
+        def mul(b):
+            t = work.tile([P, NG, P, 2, 2], BF16, name="f_grp", align_bytes=64)
+            scales = scale[:].unsqueeze(2).to_broadcast([P, NG, P, 2, 2])
+            if b in VIA_GPSIMD:
+                w = work.tile([P, NG, P, 2], F32, name="f_words", align_bytes=64)
+                nc.scalar.copy(out=w[:], in_=st["t", b][:].rearrange("p u g r -> p g r u"))
+                nc.gpsimd.tensor_tensor(
+                    out=t[:],
+                    in0=w[:].rearrange("p g r u -> p (g r u)").bitcast(BF16).rearrange("p (g r u e) -> p g r u e", g=NG, r=P, u=2),
+                    in1=scales,
+                    op=ALU.mult,
+                )
+            else:
+                nc.vector.tensor_tensor(
+                    out=t[:],
+                    in0=st["t", b][:].rearrange("p u g r -> p (u g r)").bitcast(BF16).rearrange("p (u g r e) -> p g r u e", u=2, g=NG, e=2),
+                    in1=scales,
+                    op=ALU.mult,
+                )
+            st["g", b] = t
+
+        def quant_f(b):
+            q = work.tile([P, NG * P], U32, name="f_codes", align_bytes=64, bufs=6)
+            s = work.tile([P, NG * P], U8, name="f_scales", align_bytes=64, bufs=6)
+            nc.vector.quantize_mx(out=q[:].bitcast(FP8X4), scales=s[:], in_=st["g", b][:].rearrange("p g r u e -> p (g r u e)"))
+            st["q", b] = (q, s)
+
+        def mm1(b):
+            q, s = st["q", b]
+            acc = psa.tile([P, 4, P], F32, name="agg_ps")
+            for t in range(4):
+                for g in range(NG):
+                    nc.tensor.matmul_mx(
+                        out=acc[:, t, :],
+                        lhsT=x_codes[g][:, t * P : (t + 1) * P].bitcast(FP8X4),
+                        lhsT_scale=x_scales[g][:, t * P : (t + 1) * P],
+                        rhs=q[:, g * P : (g + 1) * P].bitcast(FP8X4),
+                        rhs_scale=s[:, g * P : (g + 1) * P],
+                        start=(g == 0),
+                        stop=(g == NG - 1),
+                    )
+            st["a", b] = acc
+
+        def copy_agg(b):
+            t = work.tile([P, P, 4], BF16, name="a_grp", align_bytes=64)
+            nc.scalar.copy(out=t[:], in_=st["a", b][:].rearrange("p t m -> p m t"))
+            st["ag", b] = t
+
+        def quant_a(b):
+            q = work.tile([P, P], U32, name="a_codes", align_bytes=64)
+            s = work.tile([P, P], U8, name="a_scales", align_bytes=64)
+            nc.vector.quantize_mx(out=q[:].bitcast(FP8X4), scales=s[:], in_=st["ag", b][:].rearrange("p m t -> p (m t)"))
+            st["aq", b] = (q, s)
+
+        def mm2(b):
+            q, s = st["aq", b]
+            acc = pso.tile([P, HID], F32, name="out_ps")
+            nc.tensor.matmul_mx(
+                out=acc[:], lhsT=q[:].bitcast(FP8X4), lhsT_scale=s[:], rhs=w_codes[:].bitcast(FP8X4), rhs_scale=w_scales[:], start=True, stop=True
+            )
+            st["o", b] = acc
+
+        def parts(b):
+            n = 2 if b == NB - 1 else 1
+            return [slice(i * HID // n, (i + 1) * HID // n) for i in range(n)]
+
+        def add_bias(b):
+            st["p", b] = []
+            for c in parts(b):
+                t = work.tile([P, HID], F32, name="pre", bufs=6)
+                nc.vector.tensor_tensor(out=t[:, c], in0=st["o", b][:, c], in1=bias[:, c], op=ALU.add)
+                st["p", b].append(t)
+
+        def finish(b):
+            for c, pre in zip(parts(b), st["p", b]):
+                t = work.tile([P, HID], F32, name="res", bufs=4)
+                nc.scalar.activation(out=t[:, c], in_=pre[:, c], func=ACT.Tanh)
+                nc.sync.dma_start(out=o_view[:, b, c], in_=t[:, c])
+
+        def group_x(g, t0, t1, engine):
+            dst = x_grp[g][:, t0:t1]
+            src = x_raw[g][:].rearrange("p j (m t) -> p t m j", t=4)[:, t0:t1]
+            if engine == "S":
+                nc.scalar.copy(out=dst, in_=src)
+            elif engine == "V":
+                nc.vector.tensor_copy(out=dst, in_=src)
+            else:
+                nc.gpsimd.tensor_scalar(out=dst, in0=src, scalar1=1.0, scalar2=0.0, op0=ALU.mult, op1=ALU.add)
+
+        def quant_x(g):
+            nc.vector.quantize_mx(out=x_codes[g][:].bitcast(FP8X4), scales=x_scales[g][:], in_=x_grp[g][:].rearrange("p t m j -> p (t m j)"))
+
+        def group_w():
+            nc.gpsimd.tensor_scalar(
+                out=w_grp[:].rearrange("p (n j) -> p n j", j=4), in0=w_raw[:].rearrange("p j n -> p n j"), scalar1=1.0, scalar2=0.0, op0=ALU.mult, op1=ALU.add
+            )
+
+        def quant_w():
+            nc.vector.quantize_mx(out=w_codes[:].bitcast(FP8X4), scales=w_scales[:], in_=w_grp[:])
+
+        cast(0)
+        cast(1)
+        turn(0)
+        cast(2)
+        turn(1)
+        cast(3)
+        group_x(0, 0, 4, "G")
+        group_x(1, 2, 4, "S")
+        group_x(1, 0, 2, "G")
+        mul(0)
+        turn(2)
+        mul(1)
+        turn(3)
+        quant_f(0)
+        cast(4)
+        mul(2)
+        turn(4)
+        quant_f(1)
+        quant_x(0)
+        cast(5)
+        mul(3)
+        turn(5)
+        group_w()
+        quant_f(2)
+        quant_x(1)
+        mm1(0)
+        mm1(1)
+        cast(6)
+        mul(4)
+        mul(5)
+        copy_agg(0)
+        quant_f(3)
+        mm1(2)
+        copy_agg(1)
+        quant_w()
+        quant_a(0)
+        quant_a(1)
+        turn(6)
+        mm2(0)
+        mm2(1)
+        cast(7)
+        mul(6)
+        copy_agg(2)
+        quant_f(4)
+        turn(7)
+        mm1(3)
+        mm1(4)
+        quant_a(2)
+        mm2(2)
+        copy_agg(3)
+        add_bias(0)
+        finish(0)
+        mul(7)
+        quant_f(6)
+        mm1(6)
+        copy_agg(4)
+        quant_a(3)
+        mm2(3)
+        add_bias(1)
+        finish(1)
+        quant_f(7)
+        mm1(7)
+        quant_a(4)
+        copy_agg(6)
+        mm2(4)
+        quant_f(5)
+        mm1(5)
+        add_bias(2)
+        finish(2)
+        quant_a(6)
+        copy_agg(7)
+        mm2(6)
+        add_bias(3)
+        finish(3)
+        copy_agg(5)
+        quant_a(7)
+        mm2(7)
+        add_bias(4)
+        quant_a(5)
+        finish(4)
+        mm2(5)
+        add_bias(6)
+        finish(6)
+        add_bias(7)
+        finish(7)
+        add_bias(5)
+        finish(5)

@@ -18,7 +18,7 @@ ALU = mybir.AluOpType
 P = 128
 NB = 8
 NG = 2
-VIA_GPSIMD = (5,)
+VIA_GPSIMD = ()
 
 
 def tile_controencodnet_pa_kernel(tc, f_bytes, f_scale, x, w1, b1, out):
@@ -79,7 +79,7 @@ def tile_controencodnet_pa_kernel(tc, f_bytes, f_scale, x, w1, b1, out):
         st = {}
 
         def cast(b):
-            t = work.tile([P, NODES], BF16, name="f_bf", align_bytes=64, bufs=6)
+            t = work.tile([P, NODES], BF16, name="f_bf", align_bytes=64, bufs=8)
             if b < 2:
                 nc.vector.tensor_copy(out=t[:], in_=bytes_of(b).bitcast(FP8))
             else:
@@ -95,7 +95,7 @@ def tile_controencodnet_pa_kernel(tc, f_bytes, f_scale, x, w1, b1, out):
             st["t", b] = t
 
         def mul(b):
-            t = work.tile([P, NG, P, 2, 2], BF16, name="f_grp", align_bytes=64)
+            t = work.tile([P, NG, P, 2, 2], BF16, name="f_grp", align_bytes=64, bufs=4)
             scales = scale[:].unsqueeze(2).to_broadcast([P, NG, P, 2, 2])
             if b in VIA_GPSIMD:
                 w = work.tile([P, NG, P, 2], F32, name="f_words", align_bytes=64)
@@ -116,8 +116,8 @@ def tile_controencodnet_pa_kernel(tc, f_bytes, f_scale, x, w1, b1, out):
             st["g", b] = t
 
         def quant_f(b):
-            q = work.tile([P, NG * P], U32, name="f_codes", align_bytes=64, bufs=6)
-            s = work.tile([P, NG * P], U8, name="f_scales", align_bytes=64, bufs=6)
+            q = work.tile([P, NG * P], U32, name="f_codes", align_bytes=64, bufs=8)
+            s = work.tile([P, NG * P], U8, name="f_scales", align_bytes=64, bufs=8)
             nc.vector.quantize_mx(out=q[:].bitcast(FP8X4), scales=s[:], in_=st["g", b][:].rearrange("p g r u e -> p (g r u e)"))
             st["q", b] = (q, s)
 
@@ -138,13 +138,13 @@ def tile_controencodnet_pa_kernel(tc, f_bytes, f_scale, x, w1, b1, out):
             st["a", b] = acc
 
         def copy_agg(b):
-            t = work.tile([P, P, 4], BF16, name="a_grp", align_bytes=64)
+            t = work.tile([P, P, 4], BF16, name="a_grp", align_bytes=64, bufs=4)
             nc.scalar.copy(out=t[:], in_=st["a", b][:].rearrange("p t m -> p m t"))
             st["ag", b] = t
 
         def quant_a(b):
-            q = work.tile([P, P], U32, name="a_codes", align_bytes=64)
-            s = work.tile([P, P], U8, name="a_scales", align_bytes=64)
+            q = work.tile([P, P], U32, name="a_codes", align_bytes=64, bufs=4)
+            s = work.tile([P, P], U8, name="a_scales", align_bytes=64, bufs=4)
             nc.vector.quantize_mx(out=q[:].bitcast(FP8X4), scales=s[:], in_=st["ag", b][:].rearrange("p m t -> p (m t)"))
             st["aq", b] = (q, s)
 
@@ -156,26 +156,19 @@ def tile_controencodnet_pa_kernel(tc, f_bytes, f_scale, x, w1, b1, out):
             )
             st["o", b] = acc
 
-        def parts(b):
-            n = 2 if b == NB - 1 else 1
-            return [slice(i * HID // n, (i + 1) * HID // n) for i in range(n)]
+        def add_bias(b, lo=0, hi=HID):
+            if ("p", b) not in st:
+                st["p", b] = work.tile([P, HID], F32, name="pre", bufs=8)
+            nc.vector.tensor_tensor(out=st["p", b][:, lo:hi], in0=st["o", b][:, lo:hi], in1=bias[:, lo:hi], op=ALU.add)
 
-        def add_bias(b):
-            st["p", b] = []
-            for c in parts(b):
-                t = work.tile([P, HID], F32, name="pre", bufs=6)
-                nc.vector.tensor_tensor(out=t[:, c], in0=st["o", b][:, c], in1=bias[:, c], op=ALU.add)
-                st["p", b].append(t)
+        def finish(b, lo=0, hi=HID):
+            t = work.tile([P, HID], F32, name="res", bufs=4)
+            nc.scalar.activation(out=t[:, lo:hi], in_=st["p", b][:, lo:hi], func=ACT.Tanh)
+            nc.sync.dma_start(out=o_view[:, b, lo:hi], in_=t[:, lo:hi])
 
-        def finish(b):
-            for c, pre in zip(parts(b), st["p", b]):
-                t = work.tile([P, HID], F32, name="res", bufs=4)
-                nc.scalar.activation(out=t[:, c], in_=pre[:, c], func=ACT.Tanh)
-                nc.sync.dma_start(out=o_view[:, b, c], in_=t[:, c])
-
-        def group_x(g, t0, t1, engine):
-            dst = x_grp[g][:, t0:t1]
-            src = x_raw[g][:].rearrange("p j (m t) -> p t m j", t=4)[:, t0:t1]
+        def group_x(g, m0, m1, engine):
+            dst = x_grp[g][:, :, m0:m1]
+            src = x_raw[g][:].rearrange("p j (m t) -> p t m j", t=4)[:, :, m0:m1]
             if engine == "S":
                 nc.scalar.copy(out=dst, in_=src)
             elif engine == "V":
@@ -186,9 +179,11 @@ def tile_controencodnet_pa_kernel(tc, f_bytes, f_scale, x, w1, b1, out):
         def quant_x(g):
             nc.vector.quantize_mx(out=x_codes[g][:].bitcast(FP8X4), scales=x_scales[g][:], in_=x_grp[g][:].rearrange("p t m j -> p (t m j)"))
 
-        def group_w():
+        def group_w(n0, n1):
             nc.gpsimd.tensor_scalar(
-                out=w_grp[:].rearrange("p (n j) -> p n j", j=4), in0=w_raw[:].rearrange("p j n -> p n j"), scalar1=1.0, scalar2=0.0, op0=ALU.mult, op1=ALU.add
+                out=w_grp[:].rearrange("p (n j) -> p n j", j=4)[:, n0:n1],
+                in0=w_raw[:].rearrange("p j n -> p n j")[:, n0:n1],
+                scalar1=1.0, scalar2=0.0, op0=ALU.mult, op1=ALU.add,
             )
 
         def quant_w():
@@ -199,85 +194,91 @@ def tile_controencodnet_pa_kernel(tc, f_bytes, f_scale, x, w1, b1, out):
         turn(0)
         cast(2)
         turn(1)
-        cast(3)
-        group_x(0, 0, 4, "G")
-        group_x(1, 2, 4, "S")
-        group_x(1, 0, 2, "G")
         mul(0)
-        turn(2)
+        group_x(0, 0, 48, "G")
+        cast(3)
         mul(1)
-        turn(3)
-        quant_f(0)
+        turn(2)
+        group_x(0, 96, 128, "S")
+        group_x(0, 48, 96, "G")
         cast(4)
-        mul(2)
-        turn(4)
+        quant_f(0)
+        turn(3)
         quant_f(1)
         quant_x(0)
+        group_x(1, 48, 128, "S")
+        group_w(0, 192)
+        mul(2)
         cast(5)
         mul(3)
-        turn(5)
-        group_w()
-        quant_f(2)
-        quant_x(1)
-        mm1(0)
-        mm1(1)
+        group_x(1, 0, 48, "G")
+        turn(4)
         cast(6)
+        quant_x(1)
+        turn(5)
+        group_w(192, 384)
         mul(4)
+        cast(7)
+        mm1(0)
         mul(5)
+        group_w(384, 512)
+        mm1(1)
         copy_agg(0)
+        quant_f(2)
         quant_f(3)
-        mm1(2)
+        turn(6)
         copy_agg(1)
+        quant_f(4)
         quant_w()
+        mm1(2)
+        mul(6)
+        turn(7)
+        copy_agg(2)
+        mm1(3)
         quant_a(0)
         quant_a(1)
-        turn(6)
+        quant_f(5)
         mm2(0)
-        mm2(1)
-        cast(7)
-        mul(6)
-        copy_agg(2)
-        quant_f(4)
-        turn(7)
-        mm1(3)
-        mm1(4)
-        quant_a(2)
-        mm2(2)
         copy_agg(3)
-        add_bias(0)
-        finish(0)
         mul(7)
-        quant_f(6)
-        mm1(6)
+        mm1(4)
+        mm2(1)
         copy_agg(4)
-        quant_a(3)
-        mm2(3)
-        add_bias(1)
-        finish(1)
+        mm1(5)
+        quant_f(6)
+        quant_a(2)
         quant_f(7)
+        mm2(2)
+        copy_agg(5)
+        add_bias(0)
+        mm1(6)
+        quant_a(3)
+        finish(0)
+        add_bias(1)
+        mm2(3)
+        copy_agg(6)
         mm1(7)
         quant_a(4)
-        copy_agg(6)
-        mm2(4)
-        quant_f(5)
-        mm1(5)
         add_bias(2)
-        finish(2)
-        quant_a(6)
-        copy_agg(7)
-        mm2(6)
-        add_bias(3)
-        finish(3)
-        copy_agg(5)
-        quant_a(7)
-        mm2(7)
-        add_bias(4)
+        finish(1)
+        mm2(4)
         quant_a(5)
-        finish(4)
+        add_bias(3)
+        copy_agg(7)
         mm2(5)
-        add_bias(6)
-        finish(6)
-        add_bias(7)
-        finish(7)
+        quant_a(6)
+        finish(2)
+        add_bias(4)
+        mm2(6)
+        finish(3)
+        quant_a(7)
         add_bias(5)
+        mm2(7)
+        finish(4)
+        add_bias(6)
         finish(5)
+        add_bias(7, 0, HID // 2)
+        finish(6)
+        add_bias(7, HID // 2, HID)
+        finish(7, 0, HID // 2)
+        finish(7, HID // 2, HID)

@@ -179,12 +179,13 @@ def tile_controencodnet_pa_kernel(tc, f_bytes, f_scale, x, w1, b1, out):
         def quant_x(g):
             nc.vector.quantize_mx(out=x_codes[g][:].bitcast(FP8X4), scales=x_scales[g][:], in_=x_grp[g][:].rearrange("p t m j -> p (t m j)"))
 
-        def group_w(n0, n1):
-            nc.gpsimd.tensor_scalar(
-                out=w_grp[:].rearrange("p (n j) -> p n j", j=4)[:, n0:n1],
-                in0=w_raw[:].rearrange("p j n -> p n j")[:, n0:n1],
-                scalar1=1.0, scalar2=0.0, op0=ALU.mult, op1=ALU.add,
-            )
+        def group_w(n0, n1, engine):
+            dst = w_grp[:].rearrange("p (n j) -> p n j", j=4)[:, n0:n1]
+            src = w_raw[:].rearrange("p j n -> p n j")[:, n0:n1]
+            if engine == "S":
+                nc.scalar.copy(out=dst, in_=src)
+            else:
+                nc.gpsimd.tensor_scalar(out=dst, in0=src, scalar1=1.0, scalar2=0.0, op0=ALU.mult, op1=ALU.add)
 
         def quant_w():
             nc.vector.quantize_mx(out=w_codes[:].bitcast(FP8X4), scales=w_scales[:], in_=w_grp[:])
@@ -196,89 +197,87 @@ def tile_controencodnet_pa_kernel(tc, f_bytes, f_scale, x, w1, b1, out):
         turn(1)
         mul(0)
         group_x(0, 0, 48, "G")
-        cast(3)
+        group_x(0, 48, 128, "S")
         mul(1)
         turn(2)
-        group_x(0, 96, 128, "S")
-        group_x(0, 48, 96, "G")
-        cast(4)
-        quant_f(0)
-        turn(3)
-        quant_f(1)
-        quant_x(0)
-        group_x(1, 48, 128, "S")
-        group_w(0, 192)
-        mul(2)
-        cast(5)
-        mul(3)
         group_x(1, 0, 48, "G")
+        cast(3)
+        quant_x(0)
+        cast(4)
+        mul(2)
+        turn(3)
+        group_w(0, 192, "G")
+        group_x(1, 48, 128, "S")
         turn(4)
-        cast(6)
+        mul(3)
+        quant_f(0)
+        cast(5)
         quant_x(1)
-        turn(5)
-        group_w(192, 384)
         mul(4)
-        cast(7)
+        group_w(192, 512, "S")
+        turn(5)
+        quant_f(1)
+        quant_f(2)
         mm1(0)
+        quant_f(3)
+        cast(6)
         mul(5)
-        group_w(384, 512)
         mm1(1)
         copy_agg(0)
-        quant_f(2)
-        quant_f(3)
+        quant_w()
+        quant_a(0)
+        quant_f(4)
+        quant_f(5)
         turn(6)
         copy_agg(1)
-        quant_f(4)
-        quant_w()
         mm1(2)
+        cast(7)
         mul(6)
-        turn(7)
-        copy_agg(2)
-        mm1(3)
-        quant_a(0)
-        quant_a(1)
-        quant_f(5)
         mm2(0)
+        mm1(3)
+        copy_agg(2)
+        quant_a(1)
+        add_bias(0)
+        turn(7)
         copy_agg(3)
-        mul(7)
+        quant_a(2)
+        quant_f(6)
         mm1(4)
+        finish(0)
+        mul(7)
         mm2(1)
         copy_agg(4)
         mm1(5)
-        quant_f(6)
-        quant_a(2)
-        quant_f(7)
+        add_bias(1)
         mm2(2)
         copy_agg(5)
-        add_bias(0)
+        quant_f(7)
         mm1(6)
         quant_a(3)
-        finish(0)
-        add_bias(1)
-        mm2(3)
-        copy_agg(6)
-        mm1(7)
-        quant_a(4)
         add_bias(2)
         finish(1)
+        mm2(3)
+        quant_a(4)
+        mm1(7)
+        copy_agg(6)
+        add_bias(3)
+        finish(2)
         mm2(4)
         quant_a(5)
-        add_bias(3)
-        copy_agg(7)
-        mm2(5)
-        quant_a(6)
-        finish(2)
         add_bias(4)
-        mm2(6)
+        mm2(5)
+        copy_agg(7)
+        quant_a(6)
         finish(3)
-        quant_a(7)
         add_bias(5)
-        mm2(7)
+        mm2(6)
         finish(4)
+        quant_a(7)
         add_bias(6)
+        mm2(7)
         finish(5)
         add_bias(7, 0, HID // 2)
-        finish(6)
         add_bias(7, HID // 2, HID)
+        finish(6)
         finish(7, 0, HID // 2)
         finish(7, HID // 2, HID)

from contextlib import ExitStack

import concourse.mybir as mybir
from concourse.masks import make_identity

NODES, FEATS, HID = 1024, 512, 512
FLOPS = 2 * NODES * NODES * FEATS + 2 * NODES * FEATS * HID

F32 = mybir.dt.float32
BF16 = mybir.dt.bfloat16
U32 = mybir.dt.uint32
U8 = mybir.dt.uint8
FP8 = mybir.dt.float8_e4m3fn
FP8X4 = mybir.dt.float8_e4m3fn_x4
ACT = mybir.ActivationFunctionType
ALU = mybir.AluOpType

P = 128
NB = 8
NG = 2
VIA_GPSIMD = ()


def tile_controencodnet_pa_kernel(tc, f_bytes, f_scale, x, w1, b1, out):
    nc = tc.nc
    f_view = f_bytes.rearrange("(p b) k -> p b k", b=NB)
    o_view = out.rearrange("(p b) h -> p b h", b=NB)

    with ExitStack() as ctx:
        keep = ctx.enter_context(tc.tile_pool(name="keep", bufs=1))
        work = ctx.enter_context(tc.tile_pool(name="work", bufs=3))
        pst = ctx.enter_context(tc.psum_pool(name="pst", bufs=2))
        psa = ctx.enter_context(tc.psum_pool(name="psa", bufs=2))
        pso = ctx.enter_context(tc.psum_pool(name="pso", bufs=4))
        ctx.enter_context(tc.manual_schedule())

        raw = [keep.tile([P, 1, NODES], U8, name="raw0"), keep.tile([P, 1, NODES], U8, name="raw1")]
        raw += [keep.tile([P, 2, NODES], U8, name="raw%d" % i) for i in (2, 4, 6)]

        def bytes_of(b):
            if b < 2:
                return raw[b][:, 0, :]
            return raw[1 + b // 2][:, b % 2, :]

        scale = keep.tile([P, NG, 2, 2], F32)
        nc.scalar.dma_start(
            out=scale[:].rearrange("p g u e -> p g (u e)"),
            in_=f_scale.rearrange("o (g p t) -> p (o g) t", p=P, t=4),
        )
        dummy = keep.tile([P, 1], F32)
        dummy2 = keep.tile([P, 1], F32)
        nc.vector.memset(dummy[:], 0.0)
        nc.scalar.activation(out=dummy2[:], in_=dummy[:], func=ACT.Tanh)

        nc.sync.dma_start(out=raw[0][:], in_=f_view[:, 0:1, :])
        nc.sync.dma_start(out=raw[1][:], in_=f_view[:, 1:2, :])
        nc.sync.dma_start(out=raw[2][:], in_=f_view[:, 2:4, :])
        x_raw = [keep.tile([P, 4, FEATS], BF16, name="x_raw%d" % g) for g in range(NG)]
        x_view = x.rearrange("(g p j) n -> g p j n", p=P, j=4)
        for g in range(NG):
            nc.sync.dma_start(out=x_raw[g][:], in_=x_view[g])
        nc.sync.dma_start(out=raw[3][:], in_=f_view[:, 4:6, :])
        nc.sync.dma_start(out=raw[4][:], in_=f_view[:, 6:8, :])
        w_raw = keep.tile([P, 4, HID], BF16)
        nc.sync.dma_start(out=w_raw[:], in_=w1.rearrange("(p j) n -> p j n", j=4))
        bias = keep.tile([P, HID], BF16)
        nc.sync.dma_start(out=bias[:], in_=b1.partition_broadcast(P))

        ident = keep.tile([P, P], F32)
        make_identity(nc, ident[:])

        x_codes = [keep.tile([P, FEATS], U32, name="x_codes%d" % g, align_bytes=64) for g in range(NG)]
        x_scales = [keep.tile([P, FEATS], U8, name="x_scales%d" % g, align_bytes=64) for g in range(NG)]
        x_grp = [keep.tile([P, 4, P, 4], BF16, name="x_grp%d" % g, align_bytes=64) for g in range(NG)]
        w_codes = keep.tile([P, HID], U32, align_bytes=64)
        w_scales = keep.tile([P, HID], U8, align_bytes=64)
        w_grp = keep.tile([P, 4 * HID], BF16, align_bytes=64)

        st = {}

        def cast(b):
            t = work.tile([P, NODES], BF16, name="f_bf", align_bytes=64, bufs=8)
            if b < 2:
                nc.vector.tensor_copy(out=t[:], in_=bytes_of(b).bitcast(FP8))
            else:
                nc.scalar.copy(out=t[:], in_=bytes_of(b).bitcast(FP8))
            st["c", b] = t

        def turn(b):
            t = pst.tile([P, 2, NG, P], F32, name="f_t")
            words = st["c", b][:].bitcast(F32)
            for g in range(NG):
                for u in range(2):
                    nc.tensor.transpose(t[:, u, g, :], words[:, 256 * g + u : 256 * (g + 1) : 2], ident[:])
            st["t", b] = t

        def mul(b):
            t = work.tile([P, NG, P, 2, 2], BF16, name="f_grp", align_bytes=64, bufs=4)
            scales = scale[:].unsqueeze(2).to_broadcast([P, NG, P, 2, 2])
            if b in VIA_GPSIMD:
                w = work.tile([P, NG, P, 2], F32, name="f_words", align_bytes=64)
                nc.scalar.copy(out=w[:], in_=st["t", b][:].rearrange("p u g r -> p g r u"))
                nc.gpsimd.tensor_tensor(
                    out=t[:],
                    in0=w[:].rearrange("p g r u -> p (g r u)").bitcast(BF16).rearrange("p (g r u e) -> p g r u e", g=NG, r=P, u=2),
                    in1=scales,
                    op=ALU.mult,
                )
            else:
                nc.vector.tensor_tensor(
                    out=t[:],
                    in0=st["t", b][:].rearrange("p u g r -> p (u g r)").bitcast(BF16).rearrange("p (u g r e) -> p g r u e", u=2, g=NG, e=2),
                    in1=scales,
                    op=ALU.mult,
                )
            st["g", b] = t

        def quant_f(b):
            q = work.tile([P, NG * P], U32, name="f_codes", align_bytes=64, bufs=8)
            s = work.tile([P, NG * P], U8, name="f_scales", align_bytes=64, bufs=8)
            nc.vector.quantize_mx(out=q[:].bitcast(FP8X4), scales=s[:], in_=st["g", b][:].rearrange("p g r u e -> p (g r u e)"))
            st["q", b] = (q, s)

        def mm1(b):
            q, s = st["q", b]
            acc = psa.tile([P, 4, P], F32, name="agg_ps")
            for t in range(4):
                for g in range(NG):
                    nc.tensor.matmul_mx(
                        out=acc[:, t, :],
                        lhsT=x_codes[g][:, t * P : (t + 1) * P].bitcast(FP8X4),
                        lhsT_scale=x_scales[g][:, t * P : (t + 1) * P],
                        rhs=q[:, g * P : (g + 1) * P].bitcast(FP8X4),
                        rhs_scale=s[:, g * P : (g + 1) * P],
                        start=(g == 0),
                        stop=(g == NG - 1),
                    )
            st["a", b] = acc

        def copy_agg(b):
            t = work.tile([P, P, 4], BF16, name="a_grp", align_bytes=64, bufs=4)
            nc.scalar.copy(out=t[:], in_=st["a", b][:].rearrange("p t m -> p m t"))
            st["ag", b] = t

        def quant_a(b):
            q = work.tile([P, P], U32, name="a_codes", align_bytes=64, bufs=4)
            s = work.tile([P, P], U8, name="a_scales", align_bytes=64, bufs=4)
            nc.vector.quantize_mx(out=q[:].bitcast(FP8X4), scales=s[:], in_=st["ag", b][:].rearrange("p m t -> p (m t)"))
            st["aq", b] = (q, s)

        def mm2(b):
            q, s = st["aq", b]
            acc = pso.tile([P, HID], F32, name="out_ps")
            nc.tensor.matmul_mx(
                out=acc[:], lhsT=q[:].bitcast(FP8X4), lhsT_scale=s[:], rhs=w_codes[:].bitcast(FP8X4), rhs_scale=w_scales[:], start=True, stop=True
            )
            st["o", b] = acc

        def add_bias(b, lo=0, hi=HID):
            if ("p", b) not in st:
                st["p", b] = work.tile([P, HID], F32, name="pre", bufs=8)
            nc.vector.tensor_tensor(out=st["p", b][:, lo:hi], in0=st["o", b][:, lo:hi], in1=bias[:, lo:hi], op=ALU.add)

        def finish(b, lo=0, hi=HID):
            t = work.tile([P, HID], F32, name="res", bufs=4)
            nc.scalar.activation(out=t[:, lo:hi], in_=st["p", b][:, lo:hi], func=ACT.Tanh)
            nc.sync.dma_start(out=o_view[:, b, lo:hi], in_=t[:, lo:hi])

        def group_x(g, m0, m1, engine):
            dst = x_grp[g][:, :, m0:m1]
            src = x_raw[g][:].rearrange("p j (m t) -> p t m j", t=4)[:, :, m0:m1]
            if engine == "S":
                nc.scalar.copy(out=dst, in_=src)
            elif engine == "V":
                nc.vector.tensor_copy(out=dst, in_=src)
            else:
                nc.gpsimd.tensor_scalar(out=dst, in0=src, scalar1=1.0, scalar2=0.0, op0=ALU.mult, op1=ALU.add)

        def quant_x(g):
            nc.vector.quantize_mx(out=x_codes[g][:].bitcast(FP8X4), scales=x_scales[g][:], in_=x_grp[g][:].rearrange("p t m j -> p (t m j)"))

        def group_w(n0, n1, engine):
            dst = w_grp[:].rearrange("p (n j) -> p n j", j=4)[:, n0:n1]
            src = w_raw[:].rearrange("p j n -> p n j")[:, n0:n1]
            if engine == "S":
                nc.scalar.copy(out=dst, in_=src)
            else:
                nc.gpsimd.tensor_scalar(out=dst, in0=src, scalar1=1.0, scalar2=0.0, op0=ALU.mult, op1=ALU.add)

        def quant_w():
            nc.vector.quantize_mx(out=w_codes[:].bitcast(FP8X4), scales=w_scales[:], in_=w_grp[:])

        cast(0)
        cast(1)
        turn(0)
        cast(2)
        turn(1)
        mul(0)
        group_x(0, 0, 48, "G")
        group_x(0, 48, 128, "S")
        mul(1)
        turn(2)
        group_x(1, 0, 48, "G")
        cast(3)
        quant_x(0)
        cast(4)
        mul(2)
        turn(3)
        group_w(0, 192, "G")
        group_x(1, 48, 128, "S")
        turn(4)
        mul(3)
        quant_f(0)
        cast(5)
        quant_x(1)
        mul(4)
        group_w(192, 512, "S")
        turn(5)
        quant_f(1)
        quant_f(2)
        mm1(0)
        quant_f(3)
        cast(6)
        mul(5)
        mm1(1)
        copy_agg(0)
        quant_w()
        quant_a(0)
        quant_f(4)
        quant_f(5)
        turn(6)
        copy_agg(1)
        mm1(2)
        cast(7)
        mul(6)
        mm2(0)
        mm1(3)
        copy_agg(2)
        quant_a(1)
        add_bias(0)
        turn(7)
        copy_agg(3)
        quant_a(2)
        quant_f(6)
        mm1(4)
        finish(0)
        mul(7)
        mm2(1)
        copy_agg(4)
        mm1(5)
        add_bias(1)
        mm2(2)
        copy_agg(5)
        quant_f(7)
        mm1(6)
        quant_a(3)
        add_bias(2)
        finish(1)
        mm2(3)
        quant_a(4)
        mm1(7)
        copy_agg(6)
        add_bias(3)
        finish(2)
        mm2(4)
        quant_a(5)
        add_bias(4)
        mm2(5)
        copy_agg(7)
        quant_a(6)
        finish(3)
        add_bias(5)
        mm2(6)
        finish(4)
        quant_a(7)
        add_bias(6)
        mm2(7)
        finish(5)
        add_bias(7, 0, HID // 2)
        add_bias(7, HID // 2, HID)
        finish(6)
        finish(7, 0, HID // 2)
        finish(7, HID // 2, HID)
